import numpy as np
import ml_dtypes


def mxq(x, axis, fmt="e4m3"):
    dtype, down = {"e4m3": (ml_dtypes.float8_e4m3fn, 7), "e5m2": (ml_dtypes.float8_e5m2, 14)}[fmt]
    v = np.moveaxis(np.asarray(x, np.float32).astype(ml_dtypes.bfloat16).astype(np.float64), axis, -1)
    blocks = v.reshape(v.shape[:-1] + (-1, 32))
    amax = np.abs(blocks).max(-1, keepdims=True)
    byte = np.maximum(np.where(amax > 0, np.frexp(amax)[1] - 1 + 127, 0) - down, 1)
    scale = np.exp2(byte - 127.0)
    codes = (blocks / scale).astype(np.float32).astype(dtype).astype(np.float64)
    return np.moveaxis((codes * scale).reshape(v.shape), -1, axis)


WIDE = False


def mx_kscale(k):
    if not WIDE:
        return np.ones(k)
    levels = np.array([10, -10, 5, -5, 0])
    a = np.random.permutation(np.resize(levels, k // 512 * 4)).reshape(k // 512, 4)
    idx = np.arange(k)
    return np.exp2(a[idx // 512, idx % 128 // 32])


BF16 = ml_dtypes.bfloat16


def bf(x):
    return np.asarray(x, np.float32).astype(BF16)


def f64(x):
    return np.asarray(x).astype(np.float64)


B, D, H, F, C, R = 128, 512, 16384, 256, 128, 32
EPS = 1e-12


def l2norm(x):
    n = np.sqrt((x ** 2).sum(-1, keepdims=True))
    return x / np.maximum(n, EPS)


def setup_inputs():
    s = mx_kscale(H)
    return {"features": bf(np.random.standard_normal((B, H)) * s),
            "ex_features": bf(np.random.standard_normal((D, H)) * s),
            "gW": bf(np.random.standard_normal((F, H)) / np.sqrt(H) / s[None, :]),
            "gb": bf(np.random.standard_normal(F) * 0.1)}


def reference(features, ex_features, gW, gb):
    wq = mxq(f64(gW), 1, "e4m3")
    f = (mxq(f64(features), 1, "e4m3") @ wq.T) + f64(gb)
    ex = (mxq(f64(ex_features), 1, "e4m3") @ wq.T) + f64(gb)
    return l2norm(f), l2norm(ex)

@@ -1,0 +1,176 @@
+from contextlib import ExitStack
+
+import concourse.masks as masks
+import concourse.mybir as mybir
+
+F32 = mybir.dt.float32
+BF16 = mybir.dt.bfloat16
+U32 = mybir.dt.uint32
+U8 = mybir.dt.uint8
+FP8X4 = mybir.dt.float8_e4m3fn_x4
+ACT = mybir.ActivationFunctionType
+ALU = mybir.AluOpType
+
+P = 128
+K = 16384
+F_OUT = 256
+EPS = 1e-12
+
+K_PASS = 4 * P
+PASSES = K // K_PASS
+HALVES = 2
+SLOTS = 2
+CHUNK_PASSES = 4
+CHUNK_K = CHUNK_PASSES * K_PASS
+CHUNKS = K // CHUNK_K
+
+W_TILES = (0, 1)
+PHASE_ONE_X = (2, 3, 4)
+PHASE_TWO_X = (5, 6)
+PHASE_ONE_STEP = 2
+PHASE_TWO_STEP = 4
+ACC_BANKS = 3
+TRANSPOSE_BANKS = 5
+RAW_BUFS = 28
+
+FLOPS = 2 * (128 + 512) * F_OUT * K
+
+
+def tile_minerva_detex_pa_k_kernel(tc, features, ex_features, gW, gb, out_0, out_1):
+    nc = tc.nc
+    rows_of = [gW[0:P, :], gW[P : 2 * P, :], features]
+    out_of = {2: out_0}
+    for i in range(4):
+        rows_of.append(ex_features[i * P : (i + 1) * P, :])
+        out_of[3 + i] = out_1[i * P : (i + 1) * P, :]
+
+    with ExitStack() as ctx:
+        ctx.enter_context(tc.manual_schedule())
+        consts = ctx.enter_context(tc.tile_pool(name="consts", bufs=1))
+        raws = ctx.enter_context(tc.tile_pool(name="raws", bufs=RAW_BUFS))
+        stage = ctx.enter_context(tc.tile_pool(name="stage", bufs=2 * TRANSPOSE_BANKS))
+        xq = ctx.enter_context(tc.tile_pool(name="xq", bufs=3 * PHASE_TWO_STEP))
+        tail = ctx.enter_context(tc.tile_pool(name="tail", bufs=ACC_BANKS))
+        banks = ctx.enter_context(tc.psum_pool(name="banks", bufs=TRANSPOSE_BANKS))
+        accs = ctx.enter_context(tc.psum_pool(name="accs", bufs=ACC_BANKS))
+
+        load_order = [(r, c) for c in range(CHUNKS) for r in W_TILES + PHASE_ONE_X]
+        load_order += [(r, c) for c in range(CHUNKS) for r in PHASE_TWO_X]
+        raw = {}
+
+        def load_more(count):
+            for r, c in load_order[len(raw) : len(raw) + count]:
+                chunk = raws.tile([P, CHUNK_K], BF16, name="chunk")
+                nc.sync.dma_start(out=chunk[:], in_=rows_of[r][:, c * CHUNK_K : (c + 1) * CHUNK_K])
+                raw[(r, c)] = chunk
+
+        load_more(RAW_BUFS)
+
+        ident = consts.tile([P, P], F32, name="ident")
+        masks.make_identity(nc, ident[:])
+
+        bias_row = consts.tile([P, F_OUT], BF16, name="bias_row")
+        nc.vector.memset(bias_row[:], 0.0)
+        nc.scalar.dma_start(out=bias_row[0:1, :], in_=gb.rearrange("(o f) -> o f", o=1))
+        ones = consts.tile([P, P], BF16, name="ones")
+        nc.vector.memset(ones[:], 1.0)
+        bias = consts.tile([P, F_OUT], F32, name="bias")
+
+        def spread_bias():
+            bias_bank = accs.tile([P, F_OUT], F32, name="bias_bank", tag="acc")
+            nc.tensor.matmul(out=bias_bank[:], lhsT=ones[:], rhs=bias_row[:], start=True, stop=True)
+            nc.vector.tensor_copy(out=bias[:], in_=bias_bank[:])
+
+        one = consts.tile([P, 1], F32, name="one")
+        nc.vector.memset(one[:], 1.0)
+        one_root = consts.tile([P, 1], F32, name="one_root")
+        nc.scalar.sqrt(out=one_root[:], in_=one[:])
+
+        w_codes = consts.tile([P, PASSES, F_OUT], U32, name="w_codes", align_bytes=64)
+        w_scales = consts.tile([P, PASSES, F_OUT], U8, name="w_scales", align_bytes=64)
+        x_operand = {}
+        acc = {}
+
+        def transpose_and_quantise(x_tiles, with_w, first_pass, n_passes):
+            passes = range(first_pass, first_pass + n_passes)
+            units = []
+            if with_w:
+                for g in passes:
+                    units.append(([(r, g) for r in W_TILES], w_codes[:, g, :], w_scales[:, g, :]))
+            for r in x_tiles:
+                for g in passes[::SLOTS]:
+                    x_codes = xq.tile([P, SLOTS * P], U32, name="x_codes", align_bytes=64)
+                    x_scales = xq.tile([P, SLOTS * P], U8, name="x_scales", align_bytes=64)
+                    for a in range(SLOTS):
+                        cols = slice(a * P, (a + 1) * P)
+                        x_operand[(r, g + a)] = (x_codes[:, cols], x_scales[:, cols])
+                    units.append(([(r, g + a) for a in range(SLOTS)], x_codes[:], x_scales[:]))
+
+            grouped_of = []
+            for i, (slots, codes, scales) in enumerate(units):
+                bank = banks.tile([P, SLOTS, HALVES, P], F32, name="bank")
+                for a, (r, g) in enumerate(slots):
+                    words = raw[(r, g // CHUNK_PASSES)][:].bitcast(F32)
+                    for u in range(HALVES):
+                        first = ((g % CHUNK_PASSES) * HALVES + u) * P
+                        nc.tensor.transpose(bank[:, a, u, :], words[:, first : first + P], ident[:])
+                grouped = stage.tile([P, SLOTS * P * 4], BF16, name="grouped", align_bytes=64)
+                side_by_side = grouped[:].bitcast(F32).rearrange(
+                    "p (a r u) -> p a r u", a=SLOTS, u=HALVES
+                )
+                by_half = bank[:].rearrange("p a u r -> p a r u")
+                if i == 0:
+                    nc.vector.tensor_copy(out=side_by_side, in_=by_half)
+                else:
+                    nc.scalar.copy(out=side_by_side, in_=by_half)
+                grouped_of.append(grouped)
+
+            if passes[-1] % CHUNK_PASSES == CHUNK_PASSES - 1:
+                load_more(len(x_tiles) + (len(W_TILES) if with_w else 0))
+
+            for i in list(range(1, len(units))) + [0]:
+                codes, scales = units[i][1:]
+                nc.vector.quantize_mx(out=codes.bitcast(FP8X4), scales=scales, in_=grouped_of[i][:])
+
+        def normalise_and_store(r):
+            y = tail.tile([P, F_OUT], F32, name="y")
+            nc.vector.tensor_tensor(out=y[:], in0=acc[r][:], in1=bias[:], op=ALU.add)
+            squares = tail.tile([P, F_OUT], F32, name="squares")
+            sum_sq = tail.tile([P, 1], F32, name="sum_sq")
+            nc.scalar.activation(out=squares[:], in_=y[:], func=ACT.Square, accum_out=sum_sq[:])
+            clamped = tail.tile([P, 1], F32, name="clamped")
+            nc.vector.tensor_scalar_max(out=clamped[:], in0=sum_sq[:], scalar1=EPS * EPS)
+            norm = tail.tile([P, 1], F32, name="norm")
+            nc.scalar.sqrt(out=norm[:], in_=clamped[:])
+            inverse = tail.tile([P, 1], F32, name="inverse")
+            nc.vector.reciprocal(out=inverse[:], in_=norm[:])
+            unit_rows = tail.tile([P, F_OUT], F32, name="unit_rows")
+            nc.vector.tensor_scalar_mul(out=unit_rows[:], in0=y[:], scalar1=inverse[:, 0:1])
+            nc.sync.dma_start(out=out_of[r], in_=unit_rows[:])
+
+        def multiply(x_tiles, with_w, first_pass, n_passes):
+            for r in x_tiles:
+                for g in range(first_pass, first_pass + n_passes):
+                    if g == 0:
+                        acc[r] = accs.tile([P, F_OUT], F32, name="acc")
+                    codes, scales = x_operand[(r, g)]
+                    nc.tensor.matmul_mx(
+                        out=acc[r][:],
+                        lhsT=codes.bitcast(FP8X4),
+                        lhsT_scale=scales,
+                        rhs=w_codes[:, g, :].bitcast(FP8X4),
+                        rhs_scale=w_scales[:, g, :],
+                        start=(g == 0),
+                        stop=(g == PASSES - 1),
+                    )
+                if first_pass + n_passes == PASSES:
+                    normalise_and_store(r)
+
+        steps = [(PHASE_ONE_X, True, g, PHASE_ONE_STEP) for g in range(0, PASSES, PHASE_ONE_STEP)]
+        steps += [(PHASE_TWO_X, False, g, PHASE_TWO_STEP) for g in range(0, PASSES, PHASE_TWO_STEP)]
+        transpose_and_quantise(*steps[0])
+        spread_bias()
+        for before, step in zip(steps, steps[1:]):
+            transpose_and_quantise(*step)
+            multiply(*before)
+        multiply(*steps[-1])

@@ -64,7 +64,12 @@ def tile_minerva_detex_pa_k_kernel(tc, features, ex_features, gW, gb, out_0, out
                 nc.sync.dma_start(out=chunk[:], in_=rows_of[r][:, c * CHUNK_K : (c + 1) * CHUNK_K])
                 raw[(r, c)] = chunk
 
-        load_more(RAW_BUFS)
+        for r, c in load_order[: len(W_TILES + PHASE_ONE_X)]:
+            raw[(r, c)] = raws.tile([P, CHUNK_K], BF16, name="chunk")
+        for half in (slice(0, CHUNK_K // 2), slice(CHUNK_K // 2, CHUNK_K)):
+            for r, c in load_order[: len(raw)]:
+                nc.sync.dma_start(out=raw[(r, c)][:, half], in_=rows_of[r][:, half])
+        load_more(RAW_BUFS - len(raw))
 
         ident = consts.tile([P, P], F32, name="ident")
         masks.make_identity(nc, ident[:])
@@ -106,7 +111,10 @@ def tile_minerva_detex_pa_k_kernel(tc, features, ex_features, gW, gb, out_0, out
                         x_operand[(r, g + a)] = (x_codes[:, cols], x_scales[:, cols])
                     units.append(([(r, g + a) for a in range(SLOTS)], x_codes[:], x_scales[:]))
 
-            grouped_of = []
+            def quantise(grouped, codes, scales):
+                nc.vector.quantize_mx(out=codes.bitcast(FP8X4), scales=scales, in_=grouped[:])
+
+            copied = None
             for i, (slots, codes, scales) in enumerate(units):
                 bank = banks.tile([P, SLOTS, HALVES, P], F32, name="bank")
                 for a, (r, g) in enumerate(slots):
@@ -119,34 +127,46 @@ def tile_minerva_detex_pa_k_kernel(tc, features, ex_features, gW, gb, out_0, out
                     "p (a r u) -> p a r u", a=SLOTS, u=HALVES
                 )
                 by_half = bank[:].rearrange("p a u r -> p a r u")
-                if i == 0:
+                if i == 1:
                     nc.vector.tensor_copy(out=side_by_side, in_=by_half)
                 else:
                     nc.scalar.copy(out=side_by_side, in_=by_half)
-                grouped_of.append(grouped)
+                if copied is not None:
+                    quantise(*copied)
+                copied = (grouped, codes, scales)
+            quantise(*copied)
 
             if passes[-1] % CHUNK_PASSES == CHUNK_PASSES - 1:
                 load_more(len(x_tiles) + (len(W_TILES) if with_w else 0))
 
-            for i in list(range(1, len(units))) + [0]:
-                codes, scales = units[i][1:]
-                nc.vector.quantize_mx(out=codes.bitcast(FP8X4), scales=scales, in_=grouped_of[i][:])
+        y = {}
+        small = {}
 
-        def normalise_and_store(r):
-            y = tail.tile([P, F_OUT], F32, name="y")
-            nc.vector.tensor_tensor(out=y[:], in0=acc[r][:], in1=bias[:], op=ALU.add)
-            squares = tail.tile([P, F_OUT], F32, name="squares")
-            sum_sq = tail.tile([P, 1], F32, name="sum_sq")
-            nc.scalar.activation(out=squares[:], in_=y[:], func=ACT.Square, accum_out=sum_sq[:])
-            clamped = tail.tile([P, 1], F32, name="clamped")
-            nc.vector.tensor_scalar_max(out=clamped[:], in0=sum_sq[:], scalar1=EPS * EPS)
-            norm = tail.tile([P, 1], F32, name="norm")
-            nc.scalar.sqrt(out=norm[:], in_=clamped[:])
-            inverse = tail.tile([P, 1], F32, name="inverse")
-            nc.vector.reciprocal(out=inverse[:], in_=norm[:])
-            unit_rows = tail.tile([P, F_OUT], F32, name="unit_rows")
-            nc.vector.tensor_scalar_mul(out=unit_rows[:], in0=y[:], scalar1=inverse[:, 0:1])
-            nc.sync.dma_start(out=out_of[r], in_=unit_rows[:])
+        def add_bias_and_square(x_tiles):
+            small["sum_sq"] = tail.tile([P, len(x_tiles)], F32, name="sum_sq")
+            for i, r in enumerate(x_tiles):
+                y[r] = tail.tile([P, F_OUT], F32, name="y")
+                nc.vector.tensor_tensor(out=y[r][:], in0=acc[r][:], in1=bias[:], op=ALU.add)
+                squares = tail.tile([P, F_OUT], F32, name="squares")
+                nc.scalar.activation(
+                    out=squares[:], in_=y[r][:], func=ACT.Square, accum_out=small["sum_sq"][:, i : i + 1]
+                )
+
+        def clamp_and_root(x_tiles):
+            clamped = tail.tile([P, len(x_tiles)], F32, name="clamped")
+            nc.vector.tensor_scalar_max(out=clamped[:], in0=small["sum_sq"][:], scalar1=EPS * EPS)
+            small["norm"] = tail.tile([P, len(x_tiles)], F32, name="norm")
+            nc.scalar.sqrt(out=small["norm"][:], in_=clamped[:])
+
+        def scale_and_store(x_tiles):
+            inverse = tail.tile([P, len(x_tiles)], F32, name="inverse")
+            nc.vector.reciprocal(out=inverse[:], in_=small["norm"][:])
+            for i, r in enumerate(x_tiles):
+                unit_rows = tail.tile([P, F_OUT], F32, name="unit_rows")
+                nc.vector.tensor_scalar_mul(out=unit_rows[:], in0=y[r][:], scalar1=inverse[:, i : i + 1])
+                nc.sync.dma_start(out=out_of[r], in_=unit_rows[:])
+
+        end_stages = (add_bias_and_square, clamp_and_root, scale_and_store)
 
         def multiply(x_tiles, with_w, first_pass, n_passes):
             for r in x_tiles:
@@ -163,14 +183,17 @@ def tile_minerva_detex_pa_k_kernel(tc, features, ex_features, gW, gb, out_0, out
                         start=(g == 0),
                         stop=(g == PASSES - 1),
                     )
-                if first_pass + n_passes == PASSES:
-                    normalise_and_store(r)
 
         steps = [(PHASE_ONE_X, True, g, PHASE_ONE_STEP) for g in range(0, PASSES, PHASE_ONE_STEP)]
         steps += [(PHASE_TWO_X, False, g, PHASE_TWO_STEP) for g in range(0, PASSES, PHASE_TWO_STEP)]
+        phase_one_steps = PASSES // PHASE_ONE_STEP
         transpose_and_quantise(*steps[0])
         spread_bias()
-        for before, step in zip(steps, steps[1:]):
-            transpose_and_quantise(*step)
-            multiply(*before)
+        for i in range(1, len(steps)):
+            transpose_and_quantise(*steps[i])
+            multiply(*steps[i - 1])
+            if 0 <= i - phase_one_steps < len(end_stages):
+                end_stages[i - phase_one_steps](PHASE_ONE_X)
         multiply(*steps[-1])
+        for stage_of_end in end_stages:
+            stage_of_end(PHASE_TWO_X)

@@ -45,7 +45,6 @@ def tile_minerva_detex_pa_k_kernel(tc, features, ex_features, gW, gb, out_0, out
         out_of[3 + i] = out_1[i * P : (i + 1) * P, :]
 
     with ExitStack() as ctx:
-        ctx.enter_context(tc.manual_schedule())
         consts = ctx.enter_context(tc.tile_pool(name="consts", bufs=1))
         raws = ctx.enter_context(tc.tile_pool(name="raws", bufs=RAW_BUFS))
         stage = ctx.enter_context(tc.tile_pool(name="stage", bufs=2 * TRANSPOSE_BANKS))

@@ -14,9 +14,11 @@ ALU = mybir.AluOpType
 P = 128
 K = 16384
 F_OUT = 256
+EX_TILES = 4
 EPS = 1e-12
 
-K_PASS = 4 * P
+PACK = 4
+K_PASS = PACK * P
 PASSES = K // K_PASS
 HALVES = 2
 SLOTS = 2
@@ -30,45 +32,59 @@ PHASE_TWO_X = (5, 6)
 PHASE_ONE_STEP = 2
 PHASE_TWO_STEP = 4
 ACC_BANKS = 3
-TRANSPOSE_BANKS = 5
-RAW_BUFS = 28
+TRANSPOSE_BANKS = 8 - ACC_BANKS
+SETS_AHEAD = 4
+PIECES_AT_ENDS = CHUNK_PASSES // PHASE_ONE_STEP
 
-FLOPS = 2 * (128 + 512) * F_OUT * K
+FLOPS = 2 * (1 + EX_TILES) * P * F_OUT * K
 
 
 def tile_minerva_detex_pa_k_kernel(tc, features, ex_features, gW, gb, out_0, out_1):
     nc = tc.nc
     rows_of = [gW[0:P, :], gW[P : 2 * P, :], features]
     out_of = {2: out_0}
-    for i in range(4):
+    for i in range(EX_TILES):
+        out_of[len(rows_of)] = out_1[i * P : (i + 1) * P, :]
         rows_of.append(ex_features[i * P : (i + 1) * P, :])
-        out_of[3 + i] = out_1[i * P : (i + 1) * P, :]
 
     with ExitStack() as ctx:
+        ctx.enter_context(tc.manual_schedule())
         consts = ctx.enter_context(tc.tile_pool(name="consts", bufs=1))
-        raws = ctx.enter_context(tc.tile_pool(name="raws", bufs=RAW_BUFS))
+        raws = ctx.enter_context(
+            tc.tile_pool(name="raws", bufs=(SETS_AHEAD + 1) * len(W_TILES + PHASE_ONE_X))
+        )
         stage = ctx.enter_context(tc.tile_pool(name="stage", bufs=2 * TRANSPOSE_BANKS))
         xq = ctx.enter_context(tc.tile_pool(name="xq", bufs=3 * PHASE_TWO_STEP))
-        tail = ctx.enter_context(tc.tile_pool(name="tail", bufs=ACC_BANKS))
+        tail = ctx.enter_context(tc.tile_pool(name="tail", bufs=len(PHASE_ONE_X)))
         banks = ctx.enter_context(tc.psum_pool(name="banks", bufs=TRANSPOSE_BANKS))
         accs = ctx.enter_context(tc.psum_pool(name="accs", bufs=ACC_BANKS))
 
-        load_order = [(r, c) for c in range(CHUNKS) for r in W_TILES + PHASE_ONE_X]
-        load_order += [(r, c) for c in range(CHUNKS) for r in PHASE_TWO_X]
+        load_sets = []
+        for c in range(CHUNKS):
+            at_an_end = c == 0 or c == CHUNKS - 1
+            load_sets.append((W_TILES + PHASE_ONE_X, c, PIECES_AT_ENDS if at_an_end else 1))
+        for c in range(CHUNKS):
+            load_sets.append((PHASE_TWO_X, c, 1))
         raw = {}
+        sets_loaded = []
 
-        def load_more(count):
-            for r, c in load_order[len(raw) : len(raw) + count]:
-                chunk = raws.tile([P, CHUNK_K], BF16, name="chunk")
-                nc.sync.dma_start(out=chunk[:], in_=rows_of[r][:, c * CHUNK_K : (c + 1) * CHUNK_K])
-                raw[(r, c)] = chunk
+        def load_next_set():
+            if len(sets_loaded) == len(load_sets):
+                return
+            row_tiles, c, pieces = load_sets[len(sets_loaded)]
+            sets_loaded.append(c)
+            for r in row_tiles:
+                raw[(r, c)] = raws.tile([P, CHUNK_K], BF16, name="chunk")
+            for piece in range(pieces):
+                cols = slice(piece * CHUNK_K // pieces, (piece + 1) * CHUNK_K // pieces)
+                for r in row_tiles:
+                    nc.sync.dma_start(
+                        out=raw[(r, c)][:, cols],
+                        in_=rows_of[r][:, c * CHUNK_K : (c + 1) * CHUNK_K][:, cols],
+                    )
 
-        for r, c in load_order[: len(W_TILES + PHASE_ONE_X)]:
-            raw[(r, c)] = raws.tile([P, CHUNK_K], BF16, name="chunk")
-        for half in (slice(0, CHUNK_K // 2), slice(CHUNK_K // 2, CHUNK_K)):
-            for r, c in load_order[: len(raw)]:
-                nc.sync.dma_start(out=raw[(r, c)][:, half], in_=rows_of[r][:, half])
-        load_more(RAW_BUFS - len(raw))
+        for ahead in range(SETS_AHEAD):
+            load_next_set()
 
         ident = consts.tile([P, P], F32, name="ident")
         masks.make_identity(nc, ident[:])
@@ -97,6 +113,9 @@ def tile_minerva_detex_pa_k_kernel(tc, features, ex_features, gW, gb, out_0, out
 
         def transpose_and_quantise(x_tiles, with_w, first_pass, n_passes):
             passes = range(first_pass, first_pass + n_passes)
+            if first_pass % CHUNK_PASSES == 0:
+                load_next_set()
+
             units = []
             if with_w:
                 for g in passes:
@@ -121,7 +140,7 @@ def tile_minerva_detex_pa_k_kernel(tc, features, ex_features, gW, gb, out_0, out
                     for u in range(HALVES):
                         first = ((g % CHUNK_PASSES) * HALVES + u) * P
                         nc.tensor.transpose(bank[:, a, u, :], words[:, first : first + P], ident[:])
-                grouped = stage.tile([P, SLOTS * P * 4], BF16, name="grouped", align_bytes=64)
+                grouped = stage.tile([P, SLOTS * P * PACK], BF16, name="grouped", align_bytes=64)
                 side_by_side = grouped[:].bitcast(F32).rearrange(
                     "p (a r u) -> p a r u", a=SLOTS, u=HALVES
                 )
@@ -135,39 +154,7 @@ def tile_minerva_detex_pa_k_kernel(tc, features, ex_features, gW, gb, out_0, out
                 copied = (grouped, codes, scales)
             quantise(*copied)
 
-            if passes[-1] % CHUNK_PASSES == CHUNK_PASSES - 1:
-                load_more(len(x_tiles) + (len(W_TILES) if with_w else 0))
-
-        y = {}
-        small = {}
-
-        def add_bias_and_square(x_tiles):
-            small["sum_sq"] = tail.tile([P, len(x_tiles)], F32, name="sum_sq")
-            for i, r in enumerate(x_tiles):
-                y[r] = tail.tile([P, F_OUT], F32, name="y")
-                nc.vector.tensor_tensor(out=y[r][:], in0=acc[r][:], in1=bias[:], op=ALU.add)
-                squares = tail.tile([P, F_OUT], F32, name="squares")
-                nc.scalar.activation(
-                    out=squares[:], in_=y[r][:], func=ACT.Square, accum_out=small["sum_sq"][:, i : i + 1]
-                )
-
-        def clamp_and_root(x_tiles):
-            clamped = tail.tile([P, len(x_tiles)], F32, name="clamped")
-            nc.vector.tensor_scalar_max(out=clamped[:], in0=small["sum_sq"][:], scalar1=EPS * EPS)
-            small["norm"] = tail.tile([P, len(x_tiles)], F32, name="norm")
-            nc.scalar.sqrt(out=small["norm"][:], in_=clamped[:])
-
-        def scale_and_store(x_tiles):
-            inverse = tail.tile([P, len(x_tiles)], F32, name="inverse")
-            nc.vector.reciprocal(out=inverse[:], in_=small["norm"][:])
-            for i, r in enumerate(x_tiles):
-                unit_rows = tail.tile([P, F_OUT], F32, name="unit_rows")
-                nc.vector.tensor_scalar_mul(out=unit_rows[:], in0=y[r][:], scalar1=inverse[:, i : i + 1])
-                nc.sync.dma_start(out=out_of[r], in_=unit_rows[:])
-
-        end_stages = (add_bias_and_square, clamp_and_root, scale_and_store)
-
-        def multiply(x_tiles, with_w, first_pass, n_passes):
+        def multiply(x_tiles, first_pass, n_passes):
             for r in x_tiles:
                 for g in range(first_pass, first_pass + n_passes):
                     if g == 0:
@@ -183,16 +170,57 @@ def tile_minerva_detex_pa_k_kernel(tc, features, ex_features, gW, gb, out_0, out
                         stop=(g == PASSES - 1),
                     )
 
-        steps = [(PHASE_ONE_X, True, g, PHASE_ONE_STEP) for g in range(0, PASSES, PHASE_ONE_STEP)]
-        steps += [(PHASE_TWO_X, False, g, PHASE_TWO_STEP) for g in range(0, PASSES, PHASE_TWO_STEP)]
-        phase_one_steps = PASSES // PHASE_ONE_STEP
+        y = {}
+        per_row = {}
+
+        def add_bias_and_square(x_tiles):
+            per_row["sum_sq"] = tail.tile([P, len(x_tiles)], F32, name="sum_sq")
+            for i, r in enumerate(x_tiles):
+                y[r] = tail.tile([P, F_OUT], F32, name="y")
+                nc.vector.tensor_tensor(out=y[r][:], in0=acc[r][:], in1=bias[:], op=ALU.add)
+                squares = tail.tile([P, F_OUT], F32, name="squares")
+                nc.scalar.activation(
+                    out=squares[:],
+                    in_=y[r][:],
+                    func=ACT.Square,
+                    accum_out=per_row["sum_sq"][:, i : i + 1],
+                )
+
+        def clamp_and_root(x_tiles):
+            clamped = tail.tile([P, len(x_tiles)], F32, name="clamped")
+            nc.vector.tensor_scalar_max(out=clamped[:], in0=per_row["sum_sq"][:], scalar1=EPS * EPS)
+            per_row["norm"] = tail.tile([P, len(x_tiles)], F32, name="norm")
+            nc.scalar.sqrt(out=per_row["norm"][:], in_=clamped[:])
+
+        def scale_and_store(x_tiles):
+            inverse = tail.tile([P, len(x_tiles)], F32, name="inverse")
+            nc.vector.reciprocal(out=inverse[:], in_=per_row["norm"][:])
+            for i, r in enumerate(x_tiles):
+                normalised = tail.tile([P, F_OUT], F32, name="normalised")
+                nc.vector.tensor_scalar_mul(out=normalised[:], in0=y[r][:], scalar1=inverse[:, i : i + 1])
+                nc.sync.dma_start(out=out_of[r], in_=normalised[:])
+
+        steps = []
+        for first_pass in range(0, PASSES, PHASE_ONE_STEP):
+            steps.append((PHASE_ONE_X, True, first_pass, PHASE_ONE_STEP))
+        phase_one_steps = len(steps)
+        for first_pass in range(0, PASSES, PHASE_TWO_STEP):
+            steps.append((PHASE_TWO_X, False, first_pass, PHASE_TWO_STEP))
+
         transpose_and_quantise(*steps[0])
         spread_bias()
         for i in range(1, len(steps)):
             transpose_and_quantise(*steps[i])
-            multiply(*steps[i - 1])
-            if 0 <= i - phase_one_steps < len(end_stages):
-                end_stages[i - phase_one_steps](PHASE_ONE_X)
-        multiply(*steps[-1])
-        for stage_of_end in end_stages:
-            stage_of_end(PHASE_TWO_X)
+            x_tiles, with_w, first_pass, n_passes = steps[i - 1]
+            multiply(x_tiles, first_pass, n_passes)
+            if i == phase_one_steps:
+                add_bias_and_square(PHASE_ONE_X)
+            if i == phase_one_steps + 1:
+                clamp_and_root(PHASE_ONE_X)
+            if i == phase_one_steps + 2:
+                scale_and_store(PHASE_ONE_X)
+        x_tiles, with_w, first_pass, n_passes = steps[-1]
+        multiply(x_tiles, first_pass, n_passes)
+        add_bias_and_square(PHASE_TWO_X)
+        clamp_and_root(PHASE_TWO_X)
+        scale_and_store(PHASE_TWO_X)

from contextlib import ExitStack

import concourse.masks as masks
import concourse.mybir as mybir

F32 = mybir.dt.float32
BF16 = mybir.dt.bfloat16
U32 = mybir.dt.uint32
U8 = mybir.dt.uint8
FP8X4 = mybir.dt.float8_e4m3fn_x4
ACT = mybir.ActivationFunctionType
ALU = mybir.AluOpType

P = 128
K = 16384
F_OUT = 256
EX_TILES = 4
EPS = 1e-12

PACK = 4
K_PASS = PACK * P
PASSES = K // K_PASS
HALVES = 2
SLOTS = 2
CHUNK_PASSES = 4
CHUNK_K = CHUNK_PASSES * K_PASS
CHUNKS = K // CHUNK_K

W_TILES = (0, 1)
PHASE_ONE_X = (2, 3, 4)
PHASE_TWO_X = (5, 6)
PHASE_ONE_STEP = 2
PHASE_TWO_STEP = 4
ACC_BANKS = 3
TRANSPOSE_BANKS = 8 - ACC_BANKS
SETS_AHEAD = 4
PIECES_AT_ENDS = CHUNK_PASSES // PHASE_ONE_STEP

FLOPS = 2 * (1 + EX_TILES) * P * F_OUT * K


def tile_minerva_detex_pa_k_kernel(tc, features, ex_features, gW, gb, out_0, out_1):
    nc = tc.nc
    rows_of = [gW[0:P, :], gW[P : 2 * P, :], features]
    out_of = {2: out_0}
    for i in range(EX_TILES):
        out_of[len(rows_of)] = out_1[i * P : (i + 1) * P, :]
        rows_of.append(ex_features[i * P : (i + 1) * P, :])

    with ExitStack() as ctx:
        ctx.enter_context(tc.manual_schedule())
        consts = ctx.enter_context(tc.tile_pool(name="consts", bufs=1))
        raws = ctx.enter_context(
            tc.tile_pool(name="raws", bufs=(SETS_AHEAD + 1) * len(W_TILES + PHASE_ONE_X))
        )
        stage = ctx.enter_context(tc.tile_pool(name="stage", bufs=2 * TRANSPOSE_BANKS))
        xq = ctx.enter_context(tc.tile_pool(name="xq", bufs=3 * PHASE_TWO_STEP))
        tail = ctx.enter_context(tc.tile_pool(name="tail", bufs=len(PHASE_ONE_X)))
        banks = ctx.enter_context(tc.psum_pool(name="banks", bufs=TRANSPOSE_BANKS))
        accs = ctx.enter_context(tc.psum_pool(name="accs", bufs=ACC_BANKS))

        load_sets = []
        for c in range(CHUNKS):
            at_an_end = c == 0 or c == CHUNKS - 1
            load_sets.append((W_TILES + PHASE_ONE_X, c, PIECES_AT_ENDS if at_an_end else 1))
        for c in range(CHUNKS):
            load_sets.append((PHASE_TWO_X, c, 1))
        raw = {}
        sets_loaded = []

        def load_next_set():
            if len(sets_loaded) == len(load_sets):
                return
            row_tiles, c, pieces = load_sets[len(sets_loaded)]
            sets_loaded.append(c)
            for r in row_tiles:
                raw[(r, c)] = raws.tile([P, CHUNK_K], BF16, name="chunk")
            for piece in range(pieces):
                cols = slice(piece * CHUNK_K // pieces, (piece + 1) * CHUNK_K // pieces)
                for r in row_tiles:
                    nc.sync.dma_start(
                        out=raw[(r, c)][:, cols],
                        in_=rows_of[r][:, c * CHUNK_K : (c + 1) * CHUNK_K][:, cols],
                    )

        for ahead in range(SETS_AHEAD):
            load_next_set()

        ident = consts.tile([P, P], F32, name="ident")
        masks.make_identity(nc, ident[:])

        bias_row = consts.tile([P, F_OUT], BF16, name="bias_row")
        nc.vector.memset(bias_row[:], 0.0)
        nc.scalar.dma_start(out=bias_row[0:1, :], in_=gb.rearrange("(o f) -> o f", o=1))
        ones = consts.tile([P, P], BF16, name="ones")
        nc.vector.memset(ones[:], 1.0)
        bias = consts.tile([P, F_OUT], F32, name="bias")

        def spread_bias():
            bias_bank = accs.tile([P, F_OUT], F32, name="bias_bank", tag="acc")
            nc.tensor.matmul(out=bias_bank[:], lhsT=ones[:], rhs=bias_row[:], start=True, stop=True)
            nc.vector.tensor_copy(out=bias[:], in_=bias_bank[:])

        one = consts.tile([P, 1], F32, name="one")
        nc.vector.memset(one[:], 1.0)
        one_root = consts.tile([P, 1], F32, name="one_root")
        nc.scalar.sqrt(out=one_root[:], in_=one[:])

        w_codes = consts.tile([P, PASSES, F_OUT], U32, name="w_codes", align_bytes=64)
        w_scales = consts.tile([P, PASSES, F_OUT], U8, name="w_scales", align_bytes=64)
        x_operand = {}
        acc = {}

        def transpose_and_quantise(x_tiles, with_w, first_pass, n_passes):
            passes = range(first_pass, first_pass + n_passes)
            if first_pass % CHUNK_PASSES == 0:
                load_next_set()

            units = []
            if with_w:
                for g in passes:
                    units.append(([(r, g) for r in W_TILES], w_codes[:, g, :], w_scales[:, g, :]))
            for r in x_tiles:
                for g in passes[::SLOTS]:
                    x_codes = xq.tile([P, SLOTS * P], U32, name="x_codes", align_bytes=64)
                    x_scales = xq.tile([P, SLOTS * P], U8, name="x_scales", align_bytes=64)
                    for a in range(SLOTS):
                        cols = slice(a * P, (a + 1) * P)
                        x_operand[(r, g + a)] = (x_codes[:, cols], x_scales[:, cols])
                    units.append(([(r, g + a) for a in range(SLOTS)], x_codes[:], x_scales[:]))

            def quantise(grouped, codes, scales):
                nc.vector.quantize_mx(out=codes.bitcast(FP8X4), scales=scales, in_=grouped[:])

            copied = None
            for i, (slots, codes, scales) in enumerate(units):
                bank = banks.tile([P, SLOTS, HALVES, P], F32, name="bank")
                for a, (r, g) in enumerate(slots):
                    words = raw[(r, g // CHUNK_PASSES)][:].bitcast(F32)
                    for u in range(HALVES):
                        first = ((g % CHUNK_PASSES) * HALVES + u) * P
                        nc.tensor.transpose(bank[:, a, u, :], words[:, first : first + P], ident[:])
                grouped = stage.tile([P, SLOTS * P * PACK], BF16, name="grouped", align_bytes=64)
                side_by_side = grouped[:].bitcast(F32).rearrange(
                    "p (a r u) -> p a r u", a=SLOTS, u=HALVES
                )
                by_half = bank[:].rearrange("p a u r -> p a r u")
                if i == 1:
                    nc.vector.tensor_copy(out=side_by_side, in_=by_half)
                else:
                    nc.scalar.copy(out=side_by_side, in_=by_half)
                if copied is not None:
                    quantise(*copied)
                copied = (grouped, codes, scales)
            quantise(*copied)

        def multiply(x_tiles, first_pass, n_passes):
            for r in x_tiles:
                for g in range(first_pass, first_pass + n_passes):
                    if g == 0:
                        acc[r] = accs.tile([P, F_OUT], F32, name="acc")
                    codes, scales = x_operand[(r, g)]
                    nc.tensor.matmul_mx(
                        out=acc[r][:],
                        lhsT=codes.bitcast(FP8X4),
                        lhsT_scale=scales,
                        rhs=w_codes[:, g, :].bitcast(FP8X4),
                        rhs_scale=w_scales[:, g, :],
                        start=(g == 0),
                        stop=(g == PASSES - 1),
                    )

        y = {}
        per_row = {}

        def add_bias_and_square(x_tiles):
            per_row["sum_sq"] = tail.tile([P, len(x_tiles)], F32, name="sum_sq")
            for i, r in enumerate(x_tiles):
                y[r] = tail.tile([P, F_OUT], F32, name="y")
                nc.vector.tensor_tensor(out=y[r][:], in0=acc[r][:], in1=bias[:], op=ALU.add)
                squares = tail.tile([P, F_OUT], F32, name="squares")
                nc.scalar.activation(
                    out=squares[:],
                    in_=y[r][:],
                    func=ACT.Square,
                    accum_out=per_row["sum_sq"][:, i : i + 1],
                )

        def clamp_and_root(x_tiles):
            clamped = tail.tile([P, len(x_tiles)], F32, name="clamped")
            nc.vector.tensor_scalar_max(out=clamped[:], in0=per_row["sum_sq"][:], scalar1=EPS * EPS)
            per_row["norm"] = tail.tile([P, len(x_tiles)], F32, name="norm")
            nc.scalar.sqrt(out=per_row["norm"][:], in_=clamped[:])

        def scale_and_store(x_tiles):
            inverse = tail.tile([P, len(x_tiles)], F32, name="inverse")
            nc.vector.reciprocal(out=inverse[:], in_=per_row["norm"][:])
            for i, r in enumerate(x_tiles):
                normalised = tail.tile([P, F_OUT], F32, name="normalised")
                nc.vector.tensor_scalar_mul(out=normalised[:], in0=y[r][:], scalar1=inverse[:, i : i + 1])
                nc.sync.dma_start(out=out_of[r], in_=normalised[:])

        steps = []
        for first_pass in range(0, PASSES, PHASE_ONE_STEP):
            steps.append((PHASE_ONE_X, True, first_pass, PHASE_ONE_STEP))
        phase_one_steps = len(steps)
        for first_pass in range(0, PASSES, PHASE_TWO_STEP):
            steps.append((PHASE_TWO_X, False, first_pass, PHASE_TWO_STEP))

        transpose_and_quantise(*steps[0])
        spread_bias()
        for i in range(1, len(steps)):
            transpose_and_quantise(*steps[i])
            x_tiles, with_w, first_pass, n_passes = steps[i - 1]
            multiply(x_tiles, first_pass, n_passes)
            if i == phase_one_steps:
                add_bias_and_square(PHASE_ONE_X)
            if i == phase_one_steps + 1:
                clamp_and_root(PHASE_ONE_X)
            if i == phase_one_steps + 2:
                scale_and_store(PHASE_ONE_X)
        x_tiles, with_w, first_pass, n_passes = steps[-1]
        multiply(x_tiles, first_pass, n_passes)
        add_bias_and_square(PHASE_TWO_X)
        clamp_and_root(PHASE_TWO_X)
        scale_and_store(PHASE_TWO_X)
